import numpy as np
import ml_dtypes


def mxq(x, axis, fmt="e4m3"):
    dtype, down = {"e4m3": (ml_dtypes.float8_e4m3fn, 7), "e5m2": (ml_dtypes.float8_e5m2, 14)}[fmt]
    v = np.moveaxis(np.asarray(x, np.float32).astype(ml_dtypes.bfloat16).astype(np.float64), axis, -1)
    blocks = v.reshape(v.shape[:-1] + (-1, 32))
    amax = np.abs(blocks).max(-1, keepdims=True)
    byte = np.maximum(np.where(amax > 0, np.frexp(amax)[1] - 1 + 127, 0) - down, 1)
    scale = np.exp2(byte - 127.0)
    codes = (blocks / scale).astype(np.float32).astype(dtype).astype(np.float64)
    return np.moveaxis((codes * scale).reshape(v.shape), -1, axis)


WIDE = False


def mx_kscale(k):
    if not WIDE:
        return np.ones(k)
    levels = np.array([10, -10, 5, -5, 0])
    a = np.random.permutation(np.resize(levels, k // 512 * 4)).reshape(k // 512, 4)
    idx = np.arange(k)
    return np.exp2(a[idx // 512, idx % 128 // 32])


BF16 = ml_dtypes.bfloat16


def bf(x):
    return np.asarray(x, np.float32).astype(BF16)


def f64(x):
    return np.asarray(x).astype(np.float64)


E2M1 = np.array([0.0, 0.5, 1.0, 1.5, 2.0, 3.0, 4.0, 6.0, -0.0, -0.5, -1.0, -1.5, -2.0, -3.0, -4.0, -6.0])


def pack_weight(w, fmt):
    k, n = w.shape
    w = f64(bf(w)).reshape(k // 32, 32, n)
    amax = np.abs(w).max(1)
    if fmt == "e4m3":
        byte = np.frexp(amax)[1] - 1 + 127 - 7
    else:
        mant, ex = np.frexp(amax / 6.0)
        byte = np.where(mant > 0.5, ex, ex - 1) + 127
    byte = np.clip(np.where(amax > 0, byte, 1), 1, 254)
    scaled = (w * np.exp2(127.0 - byte)[:, None, :]).reshape(k, n).astype(np.float32)
    by_word = np.ascontiguousarray(scaled.reshape(k // 512, 128, 4, n).transpose(0, 1, 3, 2))
    if fmt == "e4m3":
        words = by_word.astype(ml_dtypes.float8_e4m3fn).view(np.uint8)
    else:
        c = by_word.astype(ml_dtypes.float4_e2m1fn).view(np.uint8) & 0xF
        words = c[..., 0::2] | (c[..., 1::2] << 4)
    return np.ascontiguousarray(words), np.ascontiguousarray(byte.astype(np.uint8).reshape(k // 512, 16, n))


def unpack_weight(words, scales, fmt):
    g, p, n, _ = words.shape
    if fmt == "e4m3":
        vals = np.ascontiguousarray(words).view(ml_dtypes.float8_e4m3fn).astype(np.float64)
    else:
        nib = np.empty((g, p, n, 4), np.uint8)
        nib[..., 0::2] = words & 0xF
        nib[..., 1::2] = words >> 4
        vals = E2M1[nib]
    vals = vals * np.repeat(np.exp2(scales.astype(np.float64) - 127.0), 8, axis=1)[..., None]
    return vals.transpose(0, 1, 3, 2).reshape(g * 512, n)


B, I, P, F = 512, 1024, 512, 2048
FMT = "e4m3"


def setup_inputs():
    s = mx_kscale(I)
    x = bf(np.random.standard_normal((B, I)) * s)
    features_words, features_scales = pack_weight((np.random.uniform(-1.0, 1.0, (F, I)) * np.sqrt(3.0 / I) / s).T, FMT)
    prototypes_words, prototypes_scales = pack_weight((np.random.uniform(-1.0, 1.0, (P, I)) * np.sqrt(3.0) * s).T, FMT)
    return {"x": x,
            "features_words": features_words,
            "features_scales": features_scales,
            "prototypes_words": prototypes_words,
            "prototypes_scales": prototypes_scales,
            "alpha": bf((2.0 + 0.3 * np.random.standard_normal(1)) / F),
            "beta": bf((1.5 + 0.3 * np.random.standard_normal(1)) / F),
            "theta": bf((8.0 + np.random.standard_normal(1)) / F)}


def reference(x, features_words, features_scales, prototypes_words, prototypes_scales, alpha, beta, theta):
    fq = unpack_weight(features_words, features_scales, FMT).T
    pq = unpack_weight(prototypes_words, prototypes_scales, FMT).T
    xf = mxq(f64(x), 1, "e4m3") @ fq.T
    pf = pq @ fq.T
    x_pres = np.maximum(xf, 0.0)
    p_pres = np.maximum(pf, 0.0)
    a = xf * x_pres
    c = pf * p_pres
    aq = mxq(a, 1, "e4m3")
    cq = mxq(c, 1, "e4m3")
    common = aq @ cq.T
    x_distinctive = aq @ mxq(1.0 - p_pres, 1, "e4m3").T
    p_distinctive = mxq(1.0 - x_pres, 1, "e4m3") @ cq.T
    return f64(theta) * common - f64(alpha) * x_distinctive - f64(beta) * p_distinctive

@@ -1,0 +1,242 @@
+from contextlib import ExitStack
+
+import concourse.mybir as mybir
+from concourse.masks import make_identity
+
+F32 = mybir.dt.float32
+BF16 = mybir.dt.bfloat16
+I32 = mybir.dt.int32
+U32 = mybir.dt.uint32
+U8 = mybir.dt.uint8
+FP8X4 = mybir.dt.float8_e4m3fn_x4
+ALU = mybir.AluOpType
+FUNC = mybir.ActivationFunctionType
+
+P = 128
+PACK = 4
+K_PASS = P * PACK
+
+BATCH = 512
+INPUTS = 1024
+PROTOS = 512
+FEATURES = 2048
+INPUT_PASSES = INPUTS // K_PASS
+FEATURE_PASSES = FEATURES // K_PASS
+BATCH_TILES = BATCH // P
+ROUND_BANKS = 4
+ROUND_COLS = ROUND_BANKS * K_PASS
+
+SQUARES_ON_SCALAR = ROUND_COLS // 2
+
+FLOPS = 2 * FEATURES * (INPUTS * (BATCH + PROTOS) + 3 * BATCH * PROTOS)
+
+
+def load_scale_planes(nc, planes, scales):
+    for quadrant in range(4):
+        nc.sync.dma_start(
+            out=planes[32 * quadrant : 32 * quadrant + 4 * INPUT_PASSES, :].bitcast(I32),
+            in_=scales[:, 4 * quadrant : 4 * quadrant + 4, :].bitcast(I32),
+        )
+
+
+def tile_tverskylayer_pa_kernel(
+    tc,
+    x,
+    features_words,
+    features_scales,
+    prototypes_words,
+    prototypes_scales,
+    alpha,
+    beta,
+    theta,
+    out,
+):
+    nc = tc.nc
+    with ExitStack() as ctx:
+        ctx.enter_context(tc.manual_schedule())
+        keep = ctx.enter_context(tc.tile_pool(name="keep", bufs=1))
+        work = ctx.enter_context(tc.tile_pool(name="work", bufs=2))
+        first_psum = ctx.enter_context(tc.psum_pool(name="first_psum", bufs=5))
+        second_psum = ctx.enter_context(tc.psum_pool(name="second_psum", bufs=1))
+
+        x_rows = keep.tile([P, BATCH_TILES, INPUTS], BF16)
+        x_grouped = keep.tile([P, INPUT_PASSES, PACK * BATCH], BF16, align_bytes=64)
+        x_words = keep.tile([P, INPUT_PASSES, BATCH], U32, align_bytes=64)
+        x_planes = keep.tile([P, BATCH], U8, align_bytes=64)
+        proto_words = keep.tile([P, INPUT_PASSES, PROTOS], U32, align_bytes=64)
+        proto_planes = keep.tile([P, PROTOS], U8, align_bytes=64)
+        feat_words = keep.tile([P, INPUT_PASSES, FEATURES], U32, align_bytes=64)
+        feat_planes = keep.tile([P, FEATURES], U8, align_bytes=64)
+        c_words = keep.tile([P, FEATURE_PASSES, PROTOS], U32, align_bytes=64)
+        c_planes = keep.tile([P, FEATURE_PASSES, PROTOS], U8, align_bytes=64)
+        one_minus_p_words = keep.tile([P, FEATURE_PASSES, PROTOS], U32, align_bytes=64)
+        one_minus_p_planes = keep.tile([P, FEATURE_PASSES, PROTOS], U8, align_bytes=64)
+        a_words = keep.tile([P, BATCH_TILES, FEATURE_PASSES * P], U32, align_bytes=64)
+        a_planes = keep.tile([P, BATCH_TILES, FEATURE_PASSES * P], U8, align_bytes=64)
+        one_minus_x_words = keep.tile([P, BATCH_TILES, FEATURE_PASSES * P], U32, align_bytes=64)
+        one_minus_x_planes = keep.tile([P, BATCH_TILES, FEATURE_PASSES * P], U8, align_bytes=64)
+
+        nc.vector.memset(proto_planes[:].bitcast(I32), 0)
+        nc.vector.memset(feat_planes[:].bitcast(I32), 0)
+        identity = keep.tile([P, P], F32)
+        make_identity(nc, identity[:])
+
+        x_by_tile = x.rearrange("(r p) k -> p r k", p=P)
+        for half in range(2):
+            nc.sync.dma_start(
+                out=x_rows[:, 2 * half : 2 * half + 2, :], in_=x_by_tile[:, 2 * half : 2 * half + 2, :]
+            )
+        feat_words_in = features_words.rearrange("c p n t -> p c (n t)").bitcast(I32)
+        proto_words_in = prototypes_words.rearrange("c p n t -> p c (n t)").bitcast(I32)
+        nc.sync.dma_start(out=proto_words[:].bitcast(I32), in_=proto_words_in)
+        for g in range(FEATURE_PASSES):
+            cols = slice(K_PASS * g, K_PASS * (g + 1))
+            nc.sync.dma_start(out=feat_words[:, :, cols].bitcast(I32), in_=feat_words_in[:, :, cols])
+            if g == 0:
+                load_scale_planes(nc, proto_planes, prototypes_scales)
+                load_scale_planes(nc, feat_planes, features_scales)
+        theta_in = keep.tile([P, 1], BF16)
+        alpha_in = keep.tile([P, 1], BF16)
+        beta_in = keep.tile([P, 1], BF16)
+        nc.sync.dma_start(out=theta_in[:], in_=theta.partition_broadcast(P))
+        nc.sync.dma_start(out=alpha_in[:], in_=alpha.partition_broadcast(P))
+        nc.sync.dma_start(out=beta_in[:], in_=beta.partition_broadcast(P))
+
+        for half in range(2):
+            for c in range(INPUT_PASSES):
+                turned = first_psum.tile([P, 2, 2 * P], F32, tag="bank")
+                for s in range(2):
+                    pairs = x_rows[:, 2 * half + s, :].bitcast(F32)
+                    for u in range(2):
+                        nc.tensor.transpose(
+                            turned[:, u, P * s : P * (s + 1)],
+                            pairs[:, 256 * c + u : 256 * (c + 1) : 2],
+                            identity[:],
+                        )
+                grouped = x_grouped[:, c, 2 * K_PASS * half : 2 * K_PASS * (half + 1)]
+                nc.scalar.copy(
+                    out=grouped.bitcast(F32).rearrange("p (w u) -> p w u", u=2),
+                    in_=turned[:].rearrange("p u w -> p w u"),
+                )
+        for half in range(2):
+            for c in range(INPUT_PASSES):
+                rows = slice(2 * P * half, 2 * P * (half + 1))
+                nc.vector.quantize_mx(
+                    out=x_words[:, c, rows].bitcast(FP8X4),
+                    scales=x_planes[4 * c : P, rows],
+                    in_=x_grouped[:, c, 2 * K_PASS * half : 2 * K_PASS * (half + 1)],
+                )
+
+        def first_stage_round(moving_words, moving_planes, banks, square, one_minus):
+            relu = work.tile([P, ROUND_BANKS, P, PACK], F32)
+            for j, (g, columns) in enumerate(banks):
+                bank = first_psum.tile([P, PACK, P], F32, tag="bank")
+                for t in range(PACK):
+                    tile_cols = slice(K_PASS * g + P * t, K_PASS * g + P * (t + 1))
+                    for c in range(INPUT_PASSES):
+                        nc.tensor.matmul_mx(
+                            out=bank[:, t, :],
+                            lhsT=feat_words[:, c, tile_cols].bitcast(FP8X4),
+                            lhsT_scale=feat_planes[4 * c : P, tile_cols],
+                            rhs=moving_words[:, c, columns].bitcast(FP8X4),
+                            rhs_scale=moving_planes[4 * c : P, columns],
+                            start=(c == 0),
+                            stop=(c == INPUT_PASSES - 1),
+                        )
+                nc.scalar.activation(
+                    out=relu[:, j, :, :], in_=bank[:].rearrange("p t w -> p w t"), func=FUNC.Relu
+                )
+            relu_flat = relu[:].rearrange("p j w t -> p (j w t)")
+            squared = work.tile([P, ROUND_COLS], BF16, align_bytes=64)
+            complement = work.tile([P, ROUND_COLS], BF16, align_bytes=64)
+            nc.scalar.activation(
+                out=squared[:, :SQUARES_ON_SCALAR],
+                in_=relu_flat[:, :SQUARES_ON_SCALAR],
+                func=FUNC.Square,
+            )
+            nc.vector.tensor_scalar(
+                out=complement[:], in0=relu_flat, scalar1=-1.0, scalar2=1.0, op0=ALU.mult, op1=ALU.add
+            )
+            nc.vector.tensor_tensor(
+                out=squared[:, SQUARES_ON_SCALAR:],
+                in0=relu_flat[:, SQUARES_ON_SCALAR:],
+                in1=relu_flat[:, SQUARES_ON_SCALAR:],
+                op=ALU.mult,
+            )
+            nc.vector.quantize_mx(
+                out=one_minus[0].bitcast(FP8X4), scales=one_minus[1], in_=complement[:]
+            )
+            nc.vector.quantize_mx(out=square[0].bitcast(FP8X4), scales=square[1], in_=squared[:])
+
+        def product(name, stationary, moving, m):
+            acc = second_psum.tile([P, PROTOS], F32, tag=name, name=name)
+            for g in range(FEATURE_PASSES):
+                rows = slice(P * g, P * (g + 1))
+                nc.tensor.matmul_mx(
+                    out=acc[:],
+                    lhsT=stationary[0][:, m, rows].bitcast(FP8X4),
+                    lhsT_scale=stationary[1][:, m, rows],
+                    rhs=moving[0][:, g, :].bitcast(FP8X4),
+                    rhs_scale=moving[1][:, g, :],
+                    start=(g == 0),
+                    stop=(g == FEATURE_PASSES - 1),
+                )
+            return acc
+
+        def second_stage(m):
+            p_distinctive = product(
+                "p_distinctive", (one_minus_x_words, one_minus_x_planes), (c_words, c_planes), m
+            )
+            common = product("common", (a_words, a_planes), (c_words, c_planes), m)
+            x_distinctive = product(
+                "x_distinctive", (a_words, a_planes), (one_minus_p_words, one_minus_p_planes), m
+            )
+            weighted = work.tile([P, PROTOS], F32)
+            nc.scalar.activation(
+                out=weighted[:], in_=p_distinctive[:], func=FUNC.Copy, scale=minus_beta[:, 0:1]
+            )
+            nc.vector.scalar_tensor_tensor(
+                out=weighted[:],
+                in0=common[:],
+                scalar=theta_col[:, 0:1],
+                in1=weighted[:],
+                op0=ALU.mult,
+                op1=ALU.add,
+            )
+            nc.vector.scalar_tensor_tensor(
+                out=weighted[:],
+                in0=x_distinctive[:],
+                scalar=minus_alpha[:, 0:1],
+                in1=weighted[:],
+                op0=ALU.mult,
+                op1=ALU.add,
+            )
+            nc.sync.dma_start(out=out[P * m : P * (m + 1), :], in_=weighted[:])
+
+        for g in range(FEATURE_PASSES):
+            first_stage_round(
+                proto_words,
+                proto_planes,
+                [(g, slice(P * j, P * (j + 1))) for j in range(ROUND_BANKS)],
+                square=(c_words[:, g, :], c_planes[:, g, :]),
+                one_minus=(one_minus_p_words[:, g, :], one_minus_p_planes[:, g, :]),
+            )
+
+        theta_col = keep.tile([P, 1], F32)
+        minus_alpha = keep.tile([P, 1], F32)
+        minus_beta = keep.tile([P, 1], F32)
+        nc.vector.tensor_copy(out=theta_col[:], in_=theta_in[:])
+        nc.vector.tensor_scalar_mul(out=minus_alpha[:], in0=alpha_in[:], scalar1=-1.0)
+        nc.vector.tensor_scalar_mul(out=minus_beta[:], in0=beta_in[:], scalar1=-1.0)
+
+        for m in range(BATCH_TILES + 1):
+            if m < BATCH_TILES:
+                first_stage_round(
+                    x_words,
+                    x_planes,
+                    [(g, slice(P * m, P * (m + 1))) for g in range(FEATURE_PASSES)],
+                    square=(a_words[:, m, :], a_planes[:, m, :]),
+                    one_minus=(one_minus_x_words[:, m, :], one_minus_x_planes[:, m, :]),
+                )
+            if m > 0:
+                second_stage(m - 1)

@@ -23,7 +23,8 @@ FEATURES = 2048
 INPUT_PASSES = INPUTS // K_PASS
 FEATURE_PASSES = FEATURES // K_PASS
 BATCH_TILES = BATCH // P
-ROUND_BANKS = 4
+COLUMN_TILES = 4
+ROUND_BANKS = 2
 ROUND_COLS = ROUND_BANKS * K_PASS
 
 SQUARES_ON_SCALAR = ROUND_COLS // 2
@@ -55,7 +56,7 @@ def tile_tverskylayer_pa_kernel(
     with ExitStack() as ctx:
         ctx.enter_context(tc.manual_schedule())
         keep = ctx.enter_context(tc.tile_pool(name="keep", bufs=1))
-        work = ctx.enter_context(tc.tile_pool(name="work", bufs=2))
+        work = ctx.enter_context(tc.tile_pool(name="work", bufs=3))
         first_psum = ctx.enter_context(tc.psum_pool(name="first_psum", bufs=5))
         second_psum = ctx.enter_context(tc.psum_pool(name="second_psum", bufs=1))
 
@@ -86,15 +87,22 @@ def tile_tverskylayer_pa_kernel(
             nc.sync.dma_start(
                 out=x_rows[:, 2 * half : 2 * half + 2, :], in_=x_by_tile[:, 2 * half : 2 * half + 2, :]
             )
-        feat_words_in = features_words.rearrange("c p n t -> p c (n t)").bitcast(I32)
-        proto_words_in = prototypes_words.rearrange("c p n t -> p c (n t)").bitcast(I32)
-        nc.sync.dma_start(out=proto_words[:].bitcast(I32), in_=proto_words_in)
+        feat_words_in = features_words.rearrange("i p n t -> p i (n t)").bitcast(I32)
+        proto_words_in = prototypes_words.rearrange("i p n t -> p i (n t)").bitcast(I32)
         for g in range(FEATURE_PASSES):
             cols = slice(K_PASS * g, K_PASS * (g + 1))
             nc.sync.dma_start(out=feat_words[:, :, cols].bitcast(I32), in_=feat_words_in[:, :, cols])
             if g == 0:
+                first_round = slice(0, P * ROUND_BANKS)
+                later_rounds = slice(P * ROUND_BANKS, PROTOS)
+                nc.sync.dma_start(
+                    out=proto_words[:, :, first_round].bitcast(I32), in_=proto_words_in[:, :, first_round]
+                )
                 load_scale_planes(nc, proto_planes, prototypes_scales)
                 load_scale_planes(nc, feat_planes, features_scales)
+                nc.sync.dma_start(
+                    out=proto_words[:, :, later_rounds].bitcast(I32), in_=proto_words_in[:, :, later_rounds]
+                )
         theta_in = keep.tile([P, 1], BF16)
         alpha_in = keep.tile([P, 1], BF16)
         beta_in = keep.tile([P, 1], BF16)
@@ -103,28 +111,28 @@ def tile_tverskylayer_pa_kernel(
         nc.sync.dma_start(out=beta_in[:], in_=beta.partition_broadcast(P))
 
         for half in range(2):
-            for c in range(INPUT_PASSES):
+            for i in range(INPUT_PASSES):
                 turned = first_psum.tile([P, 2, 2 * P], F32, tag="bank")
                 for s in range(2):
                     pairs = x_rows[:, 2 * half + s, :].bitcast(F32)
                     for u in range(2):
                         nc.tensor.transpose(
                             turned[:, u, P * s : P * (s + 1)],
-                            pairs[:, 256 * c + u : 256 * (c + 1) : 2],
+                            pairs[:, 256 * i + u : 256 * (i + 1) : 2],
                             identity[:],
                         )
-                grouped = x_grouped[:, c, 2 * K_PASS * half : 2 * K_PASS * (half + 1)]
+                grouped = x_grouped[:, i, 2 * K_PASS * half : 2 * K_PASS * (half + 1)]
                 nc.scalar.copy(
                     out=grouped.bitcast(F32).rearrange("p (w u) -> p w u", u=2),
                     in_=turned[:].rearrange("p u w -> p w u"),
                 )
         for half in range(2):
-            for c in range(INPUT_PASSES):
+            for i in range(INPUT_PASSES):
                 rows = slice(2 * P * half, 2 * P * (half + 1))
                 nc.vector.quantize_mx(
-                    out=x_words[:, c, rows].bitcast(FP8X4),
-                    scales=x_planes[4 * c : P, rows],
-                    in_=x_grouped[:, c, 2 * K_PASS * half : 2 * K_PASS * (half + 1)],
+                    out=x_words[:, i, rows].bitcast(FP8X4),
+                    scales=x_planes[4 * i : P, rows],
+                    in_=x_grouped[:, i, 2 * K_PASS * half : 2 * K_PASS * (half + 1)],
                 )
 
         def first_stage_round(moving_words, moving_planes, banks, square, one_minus):
@@ -133,15 +141,15 @@ def tile_tverskylayer_pa_kernel(
                 bank = first_psum.tile([P, PACK, P], F32, tag="bank")
                 for t in range(PACK):
                     tile_cols = slice(K_PASS * g + P * t, K_PASS * g + P * (t + 1))
-                    for c in range(INPUT_PASSES):
+                    for i in range(INPUT_PASSES):
                         nc.tensor.matmul_mx(
                             out=bank[:, t, :],
-                            lhsT=feat_words[:, c, tile_cols].bitcast(FP8X4),
-                            lhsT_scale=feat_planes[4 * c : P, tile_cols],
-                            rhs=moving_words[:, c, columns].bitcast(FP8X4),
-                            rhs_scale=moving_planes[4 * c : P, columns],
-                            start=(c == 0),
-                            stop=(c == INPUT_PASSES - 1),
+                            lhsT=feat_words[:, i, tile_cols].bitcast(FP8X4),
+                            lhsT_scale=feat_planes[4 * i : P, tile_cols],
+                            rhs=moving_words[:, i, columns].bitcast(FP8X4),
+                            rhs_scale=moving_planes[4 * i : P, columns],
+                            start=(i == 0),
+                            stop=(i == INPUT_PASSES - 1),
                         )
                 nc.scalar.activation(
                     out=relu[:, j, :, :], in_=bank[:].rearrange("p t w -> p w t"), func=FUNC.Relu
@@ -168,29 +176,28 @@ def tile_tverskylayer_pa_kernel(
             )
             nc.vector.quantize_mx(out=square[0].bitcast(FP8X4), scales=square[1], in_=squared[:])
 
-        def product(name, stationary, moving, m):
-            acc = second_psum.tile([P, PROTOS], F32, tag=name, name=name)
-            for g in range(FEATURE_PASSES):
-                rows = slice(P * g, P * (g + 1))
-                nc.tensor.matmul_mx(
-                    out=acc[:],
-                    lhsT=stationary[0][:, m, rows].bitcast(FP8X4),
-                    lhsT_scale=stationary[1][:, m, rows],
-                    rhs=moving[0][:, g, :].bitcast(FP8X4),
-                    rhs_scale=moving[1][:, g, :],
-                    start=(g == 0),
-                    stop=(g == FEATURE_PASSES - 1),
-                )
-            return acc
-
-        def second_stage(m):
-            p_distinctive = product(
-                "p_distinctive", (one_minus_x_words, one_minus_x_planes), (c_words, c_planes), m
-            )
-            common = product("common", (a_words, a_planes), (c_words, c_planes), m)
-            x_distinctive = product(
-                "x_distinctive", (a_words, a_planes), (one_minus_p_words, one_minus_p_planes), m
-            )
+        def second_stage(m, pass_groups):
+            p_distinctive = second_psum.tile([P, PROTOS], F32)
+            common = second_psum.tile([P, PROTOS], F32)
+            x_distinctive = second_psum.tile([P, PROTOS], F32)
+            a = (a_words, a_planes)
+            one_minus_x = (one_minus_x_words, one_minus_x_planes)
+            c = (c_words, c_planes)
+            one_minus_p = (one_minus_p_words, one_minus_p_planes)
+            products = [(p_distinctive, one_minus_x, c), (common, a, c), (x_distinctive, a, one_minus_p)]
+            for group in pass_groups:
+                for acc, stationary, moving in products:
+                    for g in group:
+                        rows = slice(P * g, P * (g + 1))
+                        nc.tensor.matmul_mx(
+                            out=acc[:],
+                            lhsT=stationary[0][:, m, rows].bitcast(FP8X4),
+                            lhsT_scale=stationary[1][:, m, rows],
+                            rhs=moving[0][:, g, :].bitcast(FP8X4),
+                            rhs_scale=moving[1][:, g, :],
+                            start=(g == 0),
+                            stop=(g == FEATURE_PASSES - 1),
+                        )
             weighted = work.tile([P, PROTOS], F32)
             nc.scalar.activation(
                 out=weighted[:], in_=p_distinctive[:], func=FUNC.Copy, scale=minus_beta[:, 0:1]
@@ -213,14 +220,33 @@ def tile_tverskylayer_pa_kernel(
             )
             nc.sync.dma_start(out=out[P * m : P * (m + 1), :], in_=weighted[:])
 
-        for g in range(FEATURE_PASSES):
-            first_stage_round(
-                proto_words,
-                proto_planes,
-                [(g, slice(P * j, P * (j + 1))) for j in range(ROUND_BANKS)],
-                square=(c_words[:, g, :], c_planes[:, g, :]),
-                one_minus=(one_minus_p_words[:, g, :], one_minus_p_planes[:, g, :]),
-            )
+        def prototypes_rounds(g):
+            for first in range(0, COLUMN_TILES, ROUND_BANKS):
+                cols = slice(P * first, P * (first + ROUND_BANKS))
+                first_stage_round(
+                    proto_words,
+                    proto_planes,
+                    [(g, slice(P * j, P * (j + 1))) for j in range(first, first + ROUND_BANKS)],
+                    square=(c_words[:, g, cols], c_planes[:, g, cols]),
+                    one_minus=(one_minus_p_words[:, g, cols], one_minus_p_planes[:, g, cols]),
+                )
+
+        def batch_tile_rounds(m):
+            for first in range(0, COLUMN_TILES, ROUND_BANKS):
+                cols = slice(P * first, P * (first + ROUND_BANKS))
+                first_stage_round(
+                    x_words,
+                    x_planes,
+                    [(g, slice(P * m, P * (m + 1))) for g in range(first, first + ROUND_BANKS)],
+                    square=(a_words[:, m, cols], a_planes[:, m, cols]),
+                    one_minus=(one_minus_x_words[:, m, cols], one_minus_x_planes[:, m, cols]),
+                )
+
+        last_pass = FEATURE_PASSES - 1
+        for g in range(last_pass):
+            prototypes_rounds(g)
+        batch_tile_rounds(0)
+        prototypes_rounds(last_pass)
 
         theta_col = keep.tile([P, 1], F32)
         minus_alpha = keep.tile([P, 1], F32)
@@ -229,14 +255,9 @@ def tile_tverskylayer_pa_kernel(
         nc.vector.tensor_scalar_mul(out=minus_alpha[:], in0=alpha_in[:], scalar1=-1.0)
         nc.vector.tensor_scalar_mul(out=minus_beta[:], in0=beta_in[:], scalar1=-1.0)
 
-        for m in range(BATCH_TILES + 1):
-            if m < BATCH_TILES:
-                first_stage_round(
-                    x_words,
-                    x_planes,
-                    [(g, slice(P * m, P * (m + 1))) for g in range(FEATURE_PASSES)],
-                    square=(a_words[:, m, :], a_planes[:, m, :]),
-                    one_minus=(one_minus_x_words[:, m, :], one_minus_x_planes[:, m, :]),
-                )
-            if m > 0:
-                second_stage(m - 1)
+        batch_tile_rounds(1)
+        second_stage(0, [range(last_pass), [last_pass]])
+        for m in range(1, BATCH_TILES):
+            if m + 1 < BATCH_TILES:
+                batch_tile_rounds(m + 1)
+            second_stage(m, [range(FEATURE_PASSES)])

@@ -162,29 +162,29 @@ def tile_tverskylayer_pa_kernel(
                 in_=relu_flat[:, :SQUARES_ON_SCALAR],
                 func=FUNC.Square,
             )
-            nc.vector.tensor_scalar(
-                out=complement[:], in0=relu_flat, scalar1=-1.0, scalar2=1.0, op0=ALU.mult, op1=ALU.add
-            )
             nc.vector.tensor_tensor(
                 out=squared[:, SQUARES_ON_SCALAR:],
                 in0=relu_flat[:, SQUARES_ON_SCALAR:],
                 in1=relu_flat[:, SQUARES_ON_SCALAR:],
                 op=ALU.mult,
             )
+            nc.vector.tensor_scalar(
+                out=complement[:], in0=relu_flat, scalar1=-1.0, scalar2=1.0, op0=ALU.mult, op1=ALU.add
+            )
+            nc.vector.quantize_mx(out=square[0].bitcast(FP8X4), scales=square[1], in_=squared[:])
             nc.vector.quantize_mx(
                 out=one_minus[0].bitcast(FP8X4), scales=one_minus[1], in_=complement[:]
             )
-            nc.vector.quantize_mx(out=square[0].bitcast(FP8X4), scales=square[1], in_=squared[:])
 
         def second_stage(m, pass_groups):
-            p_distinctive = second_psum.tile([P, PROTOS], F32)
             common = second_psum.tile([P, PROTOS], F32)
+            p_distinctive = second_psum.tile([P, PROTOS], F32)
             x_distinctive = second_psum.tile([P, PROTOS], F32)
             a = (a_words, a_planes)
             one_minus_x = (one_minus_x_words, one_minus_x_planes)
             c = (c_words, c_planes)
             one_minus_p = (one_minus_p_words, one_minus_p_planes)
-            products = [(p_distinctive, one_minus_x, c), (common, a, c), (x_distinctive, a, one_minus_p)]
+            products = [(common, a, c), (p_distinctive, one_minus_x, c), (x_distinctive, a, one_minus_p)]
             for group in pass_groups:
                 for acc, stationary, moving in products:
                     for g in group:
@@ -200,25 +200,26 @@ def tile_tverskylayer_pa_kernel(
                         )
             weighted = work.tile([P, PROTOS], F32)
             nc.scalar.activation(
-                out=weighted[:], in_=p_distinctive[:], func=FUNC.Copy, scale=minus_beta[:, 0:1]
+                out=weighted[:], in_=common[:], func=FUNC.Copy, scale=theta_col[:, 0:1]
             )
             nc.vector.scalar_tensor_tensor(
                 out=weighted[:],
-                in0=common[:],
-                scalar=theta_col[:, 0:1],
+                in0=p_distinctive[:],
+                scalar=minus_beta[:, 0:1],
                 in1=weighted[:],
                 op0=ALU.mult,
                 op1=ALU.add,
             )
-            nc.vector.scalar_tensor_tensor(
-                out=weighted[:],
-                in0=x_distinctive[:],
-                scalar=minus_alpha[:, 0:1],
-                in1=weighted[:],
-                op0=ALU.mult,
-                op1=ALU.add,
-            )
-            nc.sync.dma_start(out=out[P * m : P * (m + 1), :], in_=weighted[:])
+            for cols in (slice(0, PROTOS // 2), slice(PROTOS // 2, PROTOS)):
+                nc.vector.scalar_tensor_tensor(
+                    out=weighted[:, cols],
+                    in0=x_distinctive[:, cols],
+                    scalar=minus_alpha[:, 0:1],
+                    in1=weighted[:, cols],
+                    op0=ALU.mult,
+                    op1=ALU.add,
+                )
+                nc.sync.dma_start(out=out[P * m : P * (m + 1), cols], in_=weighted[:, cols])
 
         def prototypes_rounds(g):
             for first in range(0, COLUMN_TILES, ROUND_BANKS):

@@ -54,7 +54,6 @@ def tile_tverskylayer_pa_kernel(
 ):
     nc = tc.nc
     with ExitStack() as ctx:
-        ctx.enter_context(tc.manual_schedule())
         keep = ctx.enter_context(tc.tile_pool(name="keep", bufs=1))
         work = ctx.enter_context(tc.tile_pool(name="work", bufs=3))
         first_psum = ctx.enter_context(tc.psum_pool(name="first_psum", bufs=5))

@@ -81,6 +81,8 @@ def tile_tverskylayer_pa_kernel(
         identity = keep.tile([P, P], F32)
         make_identity(nc, identity[:])
 
+        load_scale_planes(nc, proto_planes, prototypes_scales)
+        load_scale_planes(nc, feat_planes, features_scales)
         x_by_tile = x.rearrange("(r p) k -> p r k", p=P)
         for half in range(2):
             nc.sync.dma_start(
@@ -97,8 +99,6 @@ def tile_tverskylayer_pa_kernel(
                 nc.sync.dma_start(
                     out=proto_words[:, :, first_round].bitcast(I32), in_=proto_words_in[:, :, first_round]
                 )
-                load_scale_planes(nc, proto_planes, prototypes_scales)
-                load_scale_planes(nc, feat_planes, features_scales)
                 nc.sync.dma_start(
                     out=proto_words[:, :, later_rounds].bitcast(I32), in_=proto_words_in[:, :, later_rounds]
                 )

@@ -81,13 +81,6 @@ def tile_tverskylayer_pa_kernel(
         identity = keep.tile([P, P], F32)
         make_identity(nc, identity[:])
 
-        load_scale_planes(nc, proto_planes, prototypes_scales)
-        load_scale_planes(nc, feat_planes, features_scales)
-        x_by_tile = x.rearrange("(r p) k -> p r k", p=P)
-        for half in range(2):
-            nc.sync.dma_start(
-                out=x_rows[:, 2 * half : 2 * half + 2, :], in_=x_by_tile[:, 2 * half : 2 * half + 2, :]
-            )
         feat_words_in = features_words.rearrange("i p n t -> p i (n t)").bitcast(I32)
         proto_words_in = prototypes_words.rearrange("i p n t -> p i (n t)").bitcast(I32)
         for g in range(FEATURE_PASSES):
@@ -99,9 +92,17 @@ def tile_tverskylayer_pa_kernel(
                 nc.sync.dma_start(
                     out=proto_words[:, :, first_round].bitcast(I32), in_=proto_words_in[:, :, first_round]
                 )
+                load_scale_planes(nc, proto_planes, prototypes_scales)
+                load_scale_planes(nc, feat_planes, features_scales)
                 nc.sync.dma_start(
                     out=proto_words[:, :, later_rounds].bitcast(I32), in_=proto_words_in[:, :, later_rounds]
                 )
+                x_by_tile = x.rearrange("(r p) k -> p r k", p=P)
+                for half in range(2):
+                    nc.sync.dma_start(
+                        out=x_rows[:, 2 * half : 2 * half + 2, :],
+                        in_=x_by_tile[:, 2 * half : 2 * half + 2, :],
+                    )
         theta_in = keep.tile([P, 1], BF16)
         alpha_in = keep.tile([P, 1], BF16)
         beta_in = keep.tile([P, 1], BF16)
@@ -109,30 +110,31 @@ def tile_tverskylayer_pa_kernel(
         nc.sync.dma_start(out=alpha_in[:], in_=alpha.partition_broadcast(P))
         nc.sync.dma_start(out=beta_in[:], in_=beta.partition_broadcast(P))
 
-        for half in range(2):
-            for i in range(INPUT_PASSES):
-                turned = first_psum.tile([P, 2, 2 * P], F32, tag="bank")
-                for s in range(2):
-                    pairs = x_rows[:, 2 * half + s, :].bitcast(F32)
-                    for u in range(2):
-                        nc.tensor.transpose(
-                            turned[:, u, P * s : P * (s + 1)],
-                            pairs[:, 256 * i + u : 256 * (i + 1) : 2],
-                            identity[:],
-                        )
-                grouped = x_grouped[:, i, 2 * K_PASS * half : 2 * K_PASS * (half + 1)]
-                nc.scalar.copy(
-                    out=grouped.bitcast(F32).rearrange("p (w u) -> p w u", u=2),
-                    in_=turned[:].rearrange("p u w -> p w u"),
-                )
-        for half in range(2):
-            for i in range(INPUT_PASSES):
-                rows = slice(2 * P * half, 2 * P * (half + 1))
-                nc.vector.quantize_mx(
-                    out=x_words[:, i, rows].bitcast(FP8X4),
-                    scales=x_planes[4 * i : P, rows],
-                    in_=x_grouped[:, i, 2 * K_PASS * half : 2 * K_PASS * (half + 1)],
-                )
+        def prepare_x():
+            for half in range(2):
+                for i in range(INPUT_PASSES):
+                    turned = first_psum.tile([P, 2, 2 * P], F32, tag="bank")
+                    for s in range(2):
+                        pairs = x_rows[:, 2 * half + s, :].bitcast(F32)
+                        for u in range(2):
+                            nc.tensor.transpose(
+                                turned[:, u, P * s : P * (s + 1)],
+                                pairs[:, 256 * i + u : 256 * (i + 1) : 2],
+                                identity[:],
+                            )
+                    grouped = x_grouped[:, i, 2 * K_PASS * half : 2 * K_PASS * (half + 1)]
+                    nc.scalar.copy(
+                        out=grouped.bitcast(F32).rearrange("p (w u) -> p w u", u=2),
+                        in_=turned[:].rearrange("p u w -> p w u"),
+                    )
+            for half in range(2):
+                for i in range(INPUT_PASSES):
+                    rows = slice(2 * P * half, 2 * P * (half + 1))
+                    nc.vector.quantize_mx(
+                        out=x_words[:, i, rows].bitcast(FP8X4),
+                        scales=x_planes[4 * i : P, rows],
+                        in_=x_grouped[:, i, 2 * K_PASS * half : 2 * K_PASS * (half + 1)],
+                    )
 
         def first_stage_round(moving_words, moving_planes, banks, square, one_minus):
             relu = work.tile([P, ROUND_BANKS, P, PACK], F32)
@@ -243,7 +245,9 @@ def tile_tverskylayer_pa_kernel(
                 )
 
         last_pass = FEATURE_PASSES - 1
-        for g in range(last_pass):
+        prototypes_rounds(0)
+        prepare_x()
+        for g in range(1, last_pass):
             prototypes_rounds(g)
         batch_tile_rounds(0)
         prototypes_rounds(last_pass)

@@ -29,6 +29,8 @@ ROUND_COLS = ROUND_BANKS * K_PASS
 
 SQUARES_ON_SCALAR = ROUND_COLS // 2
 
+WARM_UP_MATMULS = 12
+
 FLOPS = 2 * FEATURES * (INPUTS * (BATCH + PROTOS) + 3 * BATCH * PROTOS)
 
 
@@ -80,6 +82,10 @@ def tile_tverskylayer_pa_kernel(
         nc.vector.memset(feat_planes[:].bitcast(I32), 0)
         identity = keep.tile([P, P], F32)
         make_identity(nc, identity[:])
+
+        for n in range(WARM_UP_MATMULS):
+            unread = first_psum.tile([P, P], F32, tag="bank")
+            nc.tensor.matmul(out=unread[:], lhsT=identity[:], rhs=identity[:], start=True, stop=True)
 
         feat_words_in = features_words.rearrange("i p n t -> p i (n t)").bitcast(I32)
         proto_words_in = prototypes_words.rearrange("i p n t -> p i (n t)").bitcast(I32)

@@ -29,7 +29,7 @@ ROUND_COLS = ROUND_BANKS * K_PASS
 
 SQUARES_ON_SCALAR = ROUND_COLS // 2
 
-WARM_UP_MATMULS = 12
+WARM_UP_MATMULS = 6
 
 FLOPS = 2 * FEATURES * (INPUTS * (BATCH + PROTOS) + 3 * BATCH * PROTOS)
 

@@ -89,6 +89,7 @@ def tile_tverskylayer_pa_kernel(
 
         feat_words_in = features_words.rearrange("i p n t -> p i (n t)").bitcast(I32)
         proto_words_in = prototypes_words.rearrange("i p n t -> p i (n t)").bitcast(I32)
+        x_by_tile = x.rearrange("(r p) k -> p r k", p=P)
         for g in range(FEATURE_PASSES):
             cols = slice(K_PASS * g, K_PASS * (g + 1))
             nc.sync.dma_start(out=feat_words[:, :, cols].bitcast(I32), in_=feat_words_in[:, :, cols])
@@ -103,12 +104,11 @@ def tile_tverskylayer_pa_kernel(
                 nc.sync.dma_start(
                     out=proto_words[:, :, later_rounds].bitcast(I32), in_=proto_words_in[:, :, later_rounds]
                 )
-                x_by_tile = x.rearrange("(r p) k -> p r k", p=P)
-                for half in range(2):
-                    nc.sync.dma_start(
-                        out=x_rows[:, 2 * half : 2 * half + 2, :],
-                        in_=x_by_tile[:, 2 * half : 2 * half + 2, :],
-                    )
+            elif g <= 2:
+                half = g - 1
+                nc.sync.dma_start(
+                    out=x_rows[:, 2 * half : 2 * half + 2, :], in_=x_by_tile[:, 2 * half : 2 * half + 2, :]
+                )
         theta_in = keep.tile([P, 1], BF16)
         alpha_in = keep.tile([P, 1], BF16)
         beta_in = keep.tile([P, 1], BF16)
@@ -252,8 +252,9 @@ def tile_tverskylayer_pa_kernel(
 
         last_pass = FEATURE_PASSES - 1
         prototypes_rounds(0)
+        prototypes_rounds(1)
         prepare_x()
-        for g in range(1, last_pass):
+        for g in range(2, last_pass):
             prototypes_rounds(g)
         batch_tile_rounds(0)
         prototypes_rounds(last_pass)

@@ -34,11 +34,11 @@ WARM_UP_MATMULS = 6
 FLOPS = 2 * FEATURES * (INPUTS * (BATCH + PROTOS) + 3 * BATCH * PROTOS)
 
 
-def load_scale_planes(nc, planes, scales):
+def load_scale_planes(nc, planes, scales, columns):
     for quadrant in range(4):
         nc.sync.dma_start(
-            out=planes[32 * quadrant : 32 * quadrant + 4 * INPUT_PASSES, :].bitcast(I32),
-            in_=scales[:, 4 * quadrant : 4 * quadrant + 4, :].bitcast(I32),
+            out=planes[32 * quadrant : 32 * quadrant + 4 * INPUT_PASSES, columns].bitcast(I32),
+            in_=scales[:, 4 * quadrant : 4 * quadrant + 4, columns].bitcast(I32),
         )
 
 
@@ -99,11 +99,12 @@ def tile_tverskylayer_pa_kernel(
                 nc.sync.dma_start(
                     out=proto_words[:, :, first_round].bitcast(I32), in_=proto_words_in[:, :, first_round]
                 )
-                load_scale_planes(nc, proto_planes, prototypes_scales)
-                load_scale_planes(nc, feat_planes, features_scales)
+                load_scale_planes(nc, proto_planes, prototypes_scales, slice(0, PROTOS))
+                load_scale_planes(nc, feat_planes, features_scales, cols)
                 nc.sync.dma_start(
                     out=proto_words[:, :, later_rounds].bitcast(I32), in_=proto_words_in[:, :, later_rounds]
                 )
+                load_scale_planes(nc, feat_planes, features_scales, slice(K_PASS, FEATURES))
             elif g <= 2:
                 half = g - 1
                 nc.sync.dma_start(

from contextlib import ExitStack

import concourse.mybir as mybir
from concourse.masks import make_identity

F32 = mybir.dt.float32
BF16 = mybir.dt.bfloat16
I32 = mybir.dt.int32
U32 = mybir.dt.uint32
U8 = mybir.dt.uint8
FP8X4 = mybir.dt.float8_e4m3fn_x4
ALU = mybir.AluOpType
FUNC = mybir.ActivationFunctionType

P = 128
PACK = 4
K_PASS = P * PACK

BATCH = 512
INPUTS = 1024
PROTOS = 512
FEATURES = 2048
INPUT_PASSES = INPUTS // K_PASS
FEATURE_PASSES = FEATURES // K_PASS
BATCH_TILES = BATCH // P
COLUMN_TILES = 4
ROUND_BANKS = 2
ROUND_COLS = ROUND_BANKS * K_PASS

SQUARES_ON_SCALAR = ROUND_COLS // 2

WARM_UP_MATMULS = 6

FLOPS = 2 * FEATURES * (INPUTS * (BATCH + PROTOS) + 3 * BATCH * PROTOS)


def load_scale_planes(nc, planes, scales, columns):
    for quadrant in range(4):
        nc.sync.dma_start(
            out=planes[32 * quadrant : 32 * quadrant + 4 * INPUT_PASSES, columns].bitcast(I32),
            in_=scales[:, 4 * quadrant : 4 * quadrant + 4, columns].bitcast(I32),
        )


def tile_tverskylayer_pa_kernel(
    tc,
    x,
    features_words,
    features_scales,
    prototypes_words,
    prototypes_scales,
    alpha,
    beta,
    theta,
    out,
):
    nc = tc.nc
    with ExitStack() as ctx:
        keep = ctx.enter_context(tc.tile_pool(name="keep", bufs=1))
        work = ctx.enter_context(tc.tile_pool(name="work", bufs=3))
        first_psum = ctx.enter_context(tc.psum_pool(name="first_psum", bufs=5))
        second_psum = ctx.enter_context(tc.psum_pool(name="second_psum", bufs=1))

        x_rows = keep.tile([P, BATCH_TILES, INPUTS], BF16)
        x_grouped = keep.tile([P, INPUT_PASSES, PACK * BATCH], BF16, align_bytes=64)
        x_words = keep.tile([P, INPUT_PASSES, BATCH], U32, align_bytes=64)
        x_planes = keep.tile([P, BATCH], U8, align_bytes=64)
        proto_words = keep.tile([P, INPUT_PASSES, PROTOS], U32, align_bytes=64)
        proto_planes = keep.tile([P, PROTOS], U8, align_bytes=64)
        feat_words = keep.tile([P, INPUT_PASSES, FEATURES], U32, align_bytes=64)
        feat_planes = keep.tile([P, FEATURES], U8, align_bytes=64)
        c_words = keep.tile([P, FEATURE_PASSES, PROTOS], U32, align_bytes=64)
        c_planes = keep.tile([P, FEATURE_PASSES, PROTOS], U8, align_bytes=64)
        one_minus_p_words = keep.tile([P, FEATURE_PASSES, PROTOS], U32, align_bytes=64)
        one_minus_p_planes = keep.tile([P, FEATURE_PASSES, PROTOS], U8, align_bytes=64)
        a_words = keep.tile([P, BATCH_TILES, FEATURE_PASSES * P], U32, align_bytes=64)
        a_planes = keep.tile([P, BATCH_TILES, FEATURE_PASSES * P], U8, align_bytes=64)
        one_minus_x_words = keep.tile([P, BATCH_TILES, FEATURE_PASSES * P], U32, align_bytes=64)
        one_minus_x_planes = keep.tile([P, BATCH_TILES, FEATURE_PASSES * P], U8, align_bytes=64)

        nc.vector.memset(proto_planes[:].bitcast(I32), 0)
        nc.vector.memset(feat_planes[:].bitcast(I32), 0)
        identity = keep.tile([P, P], F32)
        make_identity(nc, identity[:])

        for n in range(WARM_UP_MATMULS):
            unread = first_psum.tile([P, P], F32, tag="bank")
            nc.tensor.matmul(out=unread[:], lhsT=identity[:], rhs=identity[:], start=True, stop=True)

        feat_words_in = features_words.rearrange("i p n t -> p i (n t)").bitcast(I32)
        proto_words_in = prototypes_words.rearrange("i p n t -> p i (n t)").bitcast(I32)
        x_by_tile = x.rearrange("(r p) k -> p r k", p=P)
        for g in range(FEATURE_PASSES):
            cols = slice(K_PASS * g, K_PASS * (g + 1))
            nc.sync.dma_start(out=feat_words[:, :, cols].bitcast(I32), in_=feat_words_in[:, :, cols])
            if g == 0:
                first_round = slice(0, P * ROUND_BANKS)
                later_rounds = slice(P * ROUND_BANKS, PROTOS)
                nc.sync.dma_start(
                    out=proto_words[:, :, first_round].bitcast(I32), in_=proto_words_in[:, :, first_round]
                )
                load_scale_planes(nc, proto_planes, prototypes_scales, slice(0, PROTOS))
                load_scale_planes(nc, feat_planes, features_scales, cols)
                nc.sync.dma_start(
                    out=proto_words[:, :, later_rounds].bitcast(I32), in_=proto_words_in[:, :, later_rounds]
                )
                load_scale_planes(nc, feat_planes, features_scales, slice(K_PASS, FEATURES))
            elif g <= 2:
                half = g - 1
                nc.sync.dma_start(
                    out=x_rows[:, 2 * half : 2 * half + 2, :], in_=x_by_tile[:, 2 * half : 2 * half + 2, :]
                )
        theta_in = keep.tile([P, 1], BF16)
        alpha_in = keep.tile([P, 1], BF16)
        beta_in = keep.tile([P, 1], BF16)
        nc.sync.dma_start(out=theta_in[:], in_=theta.partition_broadcast(P))
        nc.sync.dma_start(out=alpha_in[:], in_=alpha.partition_broadcast(P))
        nc.sync.dma_start(out=beta_in[:], in_=beta.partition_broadcast(P))

        def prepare_x():
            for half in range(2):
                for i in range(INPUT_PASSES):
                    turned = first_psum.tile([P, 2, 2 * P], F32, tag="bank")
                    for s in range(2):
                        pairs = x_rows[:, 2 * half + s, :].bitcast(F32)
                        for u in range(2):
                            nc.tensor.transpose(
                                turned[:, u, P * s : P * (s + 1)],
                                pairs[:, 256 * i + u : 256 * (i + 1) : 2],
                                identity[:],
                            )
                    grouped = x_grouped[:, i, 2 * K_PASS * half : 2 * K_PASS * (half + 1)]
                    nc.scalar.copy(
                        out=grouped.bitcast(F32).rearrange("p (w u) -> p w u", u=2),
                        in_=turned[:].rearrange("p u w -> p w u"),
                    )
            for half in range(2):
                for i in range(INPUT_PASSES):
                    rows = slice(2 * P * half, 2 * P * (half + 1))
                    nc.vector.quantize_mx(
                        out=x_words[:, i, rows].bitcast(FP8X4),
                        scales=x_planes[4 * i : P, rows],
                        in_=x_grouped[:, i, 2 * K_PASS * half : 2 * K_PASS * (half + 1)],
                    )

        def first_stage_round(moving_words, moving_planes, banks, square, one_minus):
            relu = work.tile([P, ROUND_BANKS, P, PACK], F32)
            for j, (g, columns) in enumerate(banks):
                bank = first_psum.tile([P, PACK, P], F32, tag="bank")
                for t in range(PACK):
                    tile_cols = slice(K_PASS * g + P * t, K_PASS * g + P * (t + 1))
                    for i in range(INPUT_PASSES):
                        nc.tensor.matmul_mx(
                            out=bank[:, t, :],
                            lhsT=feat_words[:, i, tile_cols].bitcast(FP8X4),
                            lhsT_scale=feat_planes[4 * i : P, tile_cols],
                            rhs=moving_words[:, i, columns].bitcast(FP8X4),
                            rhs_scale=moving_planes[4 * i : P, columns],
                            start=(i == 0),
                            stop=(i == INPUT_PASSES - 1),
                        )
                nc.scalar.activation(
                    out=relu[:, j, :, :], in_=bank[:].rearrange("p t w -> p w t"), func=FUNC.Relu
                )
            relu_flat = relu[:].rearrange("p j w t -> p (j w t)")
            squared = work.tile([P, ROUND_COLS], BF16, align_bytes=64)
            complement = work.tile([P, ROUND_COLS], BF16, align_bytes=64)
            nc.scalar.activation(
                out=squared[:, :SQUARES_ON_SCALAR],
                in_=relu_flat[:, :SQUARES_ON_SCALAR],
                func=FUNC.Square,
            )
            nc.vector.tensor_tensor(
                out=squared[:, SQUARES_ON_SCALAR:],
                in0=relu_flat[:, SQUARES_ON_SCALAR:],
                in1=relu_flat[:, SQUARES_ON_SCALAR:],
                op=ALU.mult,
            )
            nc.vector.tensor_scalar(
                out=complement[:], in0=relu_flat, scalar1=-1.0, scalar2=1.0, op0=ALU.mult, op1=ALU.add
            )
            nc.vector.quantize_mx(out=square[0].bitcast(FP8X4), scales=square[1], in_=squared[:])
            nc.vector.quantize_mx(
                out=one_minus[0].bitcast(FP8X4), scales=one_minus[1], in_=complement[:]
            )

        def second_stage(m, pass_groups):
            common = second_psum.tile([P, PROTOS], F32)
            p_distinctive = second_psum.tile([P, PROTOS], F32)
            x_distinctive = second_psum.tile([P, PROTOS], F32)
            a = (a_words, a_planes)
            one_minus_x = (one_minus_x_words, one_minus_x_planes)
            c = (c_words, c_planes)
            one_minus_p = (one_minus_p_words, one_minus_p_planes)
            products = [(common, a, c), (p_distinctive, one_minus_x, c), (x_distinctive, a, one_minus_p)]
            for group in pass_groups:
                for acc, stationary, moving in products:
                    for g in group:
                        rows = slice(P * g, P * (g + 1))
                        nc.tensor.matmul_mx(
                            out=acc[:],
                            lhsT=stationary[0][:, m, rows].bitcast(FP8X4),
                            lhsT_scale=stationary[1][:, m, rows],
                            rhs=moving[0][:, g, :].bitcast(FP8X4),
                            rhs_scale=moving[1][:, g, :],
                            start=(g == 0),
                            stop=(g == FEATURE_PASSES - 1),
                        )
            weighted = work.tile([P, PROTOS], F32)
            nc.scalar.activation(
                out=weighted[:], in_=common[:], func=FUNC.Copy, scale=theta_col[:, 0:1]
            )
            nc.vector.scalar_tensor_tensor(
                out=weighted[:],
                in0=p_distinctive[:],
                scalar=minus_beta[:, 0:1],
                in1=weighted[:],
                op0=ALU.mult,
                op1=ALU.add,
            )
            for cols in (slice(0, PROTOS // 2), slice(PROTOS // 2, PROTOS)):
                nc.vector.scalar_tensor_tensor(
                    out=weighted[:, cols],
                    in0=x_distinctive[:, cols],
                    scalar=minus_alpha[:, 0:1],
                    in1=weighted[:, cols],
                    op0=ALU.mult,
                    op1=ALU.add,
                )
                nc.sync.dma_start(out=out[P * m : P * (m + 1), cols], in_=weighted[:, cols])

        def prototypes_rounds(g):
            for first in range(0, COLUMN_TILES, ROUND_BANKS):
                cols = slice(P * first, P * (first + ROUND_BANKS))
                first_stage_round(
                    proto_words,
                    proto_planes,
                    [(g, slice(P * j, P * (j + 1))) for j in range(first, first + ROUND_BANKS)],
                    square=(c_words[:, g, cols], c_planes[:, g, cols]),
                    one_minus=(one_minus_p_words[:, g, cols], one_minus_p_planes[:, g, cols]),
                )

        def batch_tile_rounds(m):
            for first in range(0, COLUMN_TILES, ROUND_BANKS):
                cols = slice(P * first, P * (first + ROUND_BANKS))
                first_stage_round(
                    x_words,
                    x_planes,
                    [(g, slice(P * m, P * (m + 1))) for g in range(first, first + ROUND_BANKS)],
                    square=(a_words[:, m, cols], a_planes[:, m, cols]),
                    one_minus=(one_minus_x_words[:, m, cols], one_minus_x_planes[:, m, cols]),
                )

        last_pass = FEATURE_PASSES - 1
        prototypes_rounds(0)
        prototypes_rounds(1)
        prepare_x()
        for g in range(2, last_pass):
            prototypes_rounds(g)
        batch_tile_rounds(0)
        prototypes_rounds(last_pass)

        theta_col = keep.tile([P, 1], F32)
        minus_alpha = keep.tile([P, 1], F32)
        minus_beta = keep.tile([P, 1], F32)
        nc.vector.tensor_copy(out=theta_col[:], in_=theta_in[:])
        nc.vector.tensor_scalar_mul(out=minus_alpha[:], in0=alpha_in[:], scalar1=-1.0)
        nc.vector.tensor_scalar_mul(out=minus_beta[:], in0=beta_in[:], scalar1=-1.0)

        batch_tile_rounds(1)
        second_stage(0, [range(last_pass), [last_pass]])
        for m in range(1, BATCH_TILES):
            if m + 1 < BATCH_TILES:
                batch_tile_rounds(m + 1)
            second_stage(m, [range(FEATURE_PASSES)])
